import numpy as np
import ml_dtypes


def mxq(x, axis, fmt="e4m3"):
    dtype, down = {"e4m3": (ml_dtypes.float8_e4m3fn, 7), "e5m2": (ml_dtypes.float8_e5m2, 14)}[fmt]
    v = np.moveaxis(np.asarray(x, np.float32).astype(ml_dtypes.bfloat16).astype(np.float64), axis, -1)
    blocks = v.reshape(v.shape[:-1] + (-1, 32))
    amax = np.abs(blocks).max(-1, keepdims=True)
    byte = np.maximum(np.where(amax > 0, np.frexp(amax)[1] - 1 + 127, 0) - down, 1)
    scale = np.exp2(byte - 127.0)
    codes = (blocks / scale).astype(np.float32).astype(dtype).astype(np.float64)
    return np.moveaxis((codes * scale).reshape(v.shape), -1, axis)


WIDE = False


def mx_kscale(k):
    if not WIDE:
        return np.ones(k)
    levels = np.array([10, -10, 5, -5, 0])
    a = np.random.permutation(np.resize(levels, k // 512 * 4)).reshape(k // 512, 4)
    idx = np.arange(k)
    return np.exp2(a[idx // 512, idx % 128 // 32])


BF16 = ml_dtypes.bfloat16


def bf(x):
    return np.asarray(x, np.float32).astype(BF16)


def f64(x):
    return np.asarray(x).astype(np.float64)


B, IN, H = 128, 16384, 512


def sigmoid(v):
    return 1.0 / (1.0 + np.exp(-v))


def setup_inputs():
    s, t = mx_kscale(IN), mx_kscale(H)
    wsc = np.sqrt(2.0 / (IN + H))
    usc = 1.0 / np.sqrt(H)
    return {"joint_h": bf(np.random.standard_normal((B, H)) * t),
            "mgn_h": bf(np.random.standard_normal((B, IN)) * s),
            "W_r": bf(np.random.standard_normal((IN, H)) * wsc / s[:, None]),
            "W_h": bf(np.random.standard_normal((IN, H)) * wsc / s[:, None]),
            "U_r": bf(np.random.standard_normal((H, H)) * usc / t[:, None]),
            "U_h": bf(np.random.standard_normal((H, H)) * usc / t[:, None]),
            "b_r": bf(np.random.standard_normal(H) * 0.5),
            "b_h": bf(np.random.standard_normal(H) * 0.5)}


def reference(joint_h, mgn_h, W_r, W_h, U_r, U_h, b_r, b_h):
    h = f64(joint_h)
    xq = mxq(f64(mgn_h), 1, "e4m3")
    r = sigmoid((xq @ mxq(f64(W_r), 0, "e4m3")) + (mxq(h, 1, "e4m3") @ mxq(f64(U_r), 0, "e4m3")) + f64(b_r))
    g = h * r
    return np.tanh((xq @ mxq(f64(W_h), 0, "e4m3")) + (mxq(g, 1, "e4m3") @ mxq(f64(U_h), 0, "e4m3")) + f64(b_h))

@@ -1,0 +1,263 @@
+from contextlib import ExitStack
+
+import concourse.mybir as mybir
+from concourse.masks import make_identity
+
+BF16 = mybir.dt.bfloat16
+F32 = mybir.dt.float32
+U32 = mybir.dt.uint32
+U8 = mybir.dt.uint8
+FP8X4 = mybir.dt.float8_e4m3fn_x4
+ACT = mybir.ActivationFunctionType
+ALU = mybir.AluOpType
+
+P = 128
+PACK = 4
+K_PASS = P * PACK
+
+B, IN, H = 128, 16384, 512
+PASSES = IN // K_PASS
+H_TILES = H // P
+
+ROUND_PASSES = 2
+ROUND_K = ROUND_PASSES * K_PASS
+ROUNDS = PASSES // ROUND_PASSES
+X_LOAD_ROUNDS = 2
+U_LOAD_ROUND = 1
+U_READY_ROUND = 3
+RUN = 4
+
+FLOPS = 2 * B * H * (2 * IN + 2 * H)
+
+
+def regroup(copy, grouped, rows):
+    copy(
+        out=grouped.rearrange("p (c i) t -> p c t i", i=RUN),
+        in_=rows.rearrange("p t (c i) -> p c t i", i=RUN),
+    )
+
+
+def tile_joint_gru_pa_k_kernel(tc, joint_h, mgn_h, W_r, W_h, U_r, U_h, b_r, b_h, out):
+    nc = tc.nc
+    with ExitStack() as stack:
+        keep = stack.enter_context(tc.tile_pool(name="keep", bufs=1))
+        x_raw_pool = stack.enter_context(tc.tile_pool(name="x_raw", bufs=4))
+        x_grouped_pool = stack.enter_context(tc.tile_pool(name="x_grouped", bufs=3))
+        w_raw_pool = stack.enter_context(tc.tile_pool(name="w_raw", bufs=8))
+        w_grouped_pool = stack.enter_context(tc.tile_pool(name="w_grouped", bufs=3))
+        w_mx_pool = stack.enter_context(tc.tile_pool(name="w_mx", bufs=3))
+        sums = stack.enter_context(tc.psum_pool(name="sums", bufs=1))
+        work = stack.enter_context(tc.psum_pool(name="work", bufs=3))
+        stack.enter_context(tc.manual_schedule())
+
+        ident_f32 = keep.tile([P, P], F32)
+        make_identity(nc, ident_f32[:])
+        ident_bf16 = keep.tile([P, P], BF16)
+        make_identity(nc, ident_bf16[:])
+        ones = keep.tile([P, P], BF16)
+        nc.vector.memset(ones[:], 1.0)
+
+        h_sb = keep.tile([B, H], BF16)
+        nc.scalar.dma_start(out=h_sb[:], in_=joint_h)
+        br_rows = keep.tile([P, P], BF16)
+        nc.vector.memset(br_rows[:], 0.0)
+        nc.scalar.dma_start(out=br_rows[0:H_TILES, :], in_=b_r.rearrange("(t p) -> t p", p=P))
+        bh_rows = keep.tile([P, H], BF16)
+        nc.vector.memset(bh_rows[:], 0.0)
+        nc.scalar.dma_start(out=bh_rows[0:1, :], in_=b_h.unsqueeze(0))
+
+        warm = keep.tile([P, 1], F32)
+        nc.vector.memset(warm[:], 0.0)
+        nc.scalar.activation(out=warm[:], in_=warm[:], func=ACT.Tanh)
+
+        rT = [sums.tile([P, B], F32, name="rT%d" % m) for m in range(H_TILES)]
+        cand = sums.tile([B, H], F32)
+
+        x_codes = keep.tile([P, PASSES * B], U32, align_bytes=64)
+        x_scales = keep.tile([P, PASSES * B], U8, align_bytes=64)
+
+        u_raw, u_grouped, u_codes, u_scales = {}, {}, {}, {}
+        for gate in ("r", "h"):
+            u_raw[gate] = keep.tile([P, PACK, H], BF16, name="u_raw_" + gate)
+            u_grouped[gate] = keep.tile([P, H, PACK], BF16, name="u_grouped_" + gate, align_bytes=64)
+            u_codes[gate] = keep.tile([P, H], U32, name="u_codes_" + gate, align_bytes=64)
+            u_scales[gate] = keep.tile([P, H], U8, name="u_scales_" + gate, align_bytes=64)
+        h_grouped = keep.tile([P, B, PACK], BF16, align_bytes=64)
+        h_codes = keep.tile([P, B], U32, align_bytes=64)
+        h_scales = keep.tile([P, B], U8, align_bytes=64)
+        half_hT = keep.tile([P, H_TILES, B], F32)
+        half_br = keep.tile([P, H_TILES], F32)
+        bh_all = keep.tile([P, H], F32)
+        tanh_rT = keep.tile([P, H_TILES, B], F32)
+        g_grouped = keep.tile([P, B, PACK], BF16, align_bytes=64)
+        g_codes = keep.tile([P, B], U32, align_bytes=64)
+        g_scales = keep.tile([P, B], U8, align_bytes=64)
+
+        def prepare_small_operands():
+            hT_ps = work.tile([P, H_TILES, B], BF16, tag="work")
+            for t in range(H_TILES):
+                nc.tensor.transpose(hT_ps[:, t, :], h_sb[:, t * P : (t + 1) * P], ident_bf16[:])
+            brT_ps = work.tile([P, P], BF16, tag="work")
+            nc.tensor.transpose(brT_ps[:], br_rows[:], ident_bf16[:])
+            bh_ps = work.tile([P, H], F32, tag="work")
+            nc.tensor.matmul(bh_ps[:], lhsT=ones[:], rhs=bh_rows[:], start=True, stop=True)
+
+            nc.vector.tensor_copy(out=h_grouped[:], in_=hT_ps[:].rearrange("p t b -> p b t"))
+            nc.scalar.mul(out=half_hT[:], in_=hT_ps[:], mul=0.5)
+            nc.scalar.mul(out=half_br[:], in_=brT_ps[:, 0:H_TILES], mul=0.5)
+            nc.scalar.copy(out=bh_all[:], in_=bh_ps[:])
+            regroup(nc.vector.tensor_copy, u_grouped["r"][:], u_raw["r"][:])
+            regroup(nc.vector.tensor_copy, u_grouped["h"][:], u_raw["h"][:])
+
+            nc.vector.quantize_mx(
+                out=h_codes[:].bitcast(FP8X4),
+                scales=h_scales[:],
+                in_=h_grouped[:].rearrange("p b t -> p (b t)"),
+            )
+            for gate in ("r", "h"):
+                nc.vector.quantize_mx(
+                    out=u_codes[gate][:].bitcast(FP8X4),
+                    scales=u_scales[gate][:],
+                    in_=u_grouped[gate][:].rearrange("p n t -> p (n t)"),
+                )
+            for m in range(H_TILES):
+                nc.tensor.matmul_mx(
+                    out=rT[m][:],
+                    lhsT=u_codes["r"][:, m * P : (m + 1) * P].bitcast(FP8X4),
+                    lhsT_scale=u_scales["r"][:, m * P : (m + 1) * P],
+                    rhs=h_codes[:].bitcast(FP8X4),
+                    rhs_scale=h_scales[:],
+                    start=False,
+                    stop=False,
+                )
+
+        def fetch_and_regroup(i, x_raw):
+            weights = W_r if i < ROUNDS else W_h
+            w_raw = []
+            for c in range(ROUND_PASSES):
+                first_row = (i % ROUNDS) * ROUND_K + c * K_PASS
+                w_raw.append(w_raw_pool.tile([P, PACK, H], BF16, name="w_raw%d" % c))
+                nc.sync.dma_start(
+                    out=w_raw[c][:],
+                    in_=weights[first_row : first_row + K_PASS, :].rearrange("(p t) n -> p t n", p=P),
+                )
+
+            w_grouped = w_grouped_pool.tile([P, ROUND_PASSES, H, PACK], BF16, align_bytes=64)
+            regroup(nc.scalar.copy, w_grouped[:, 0, :, :], w_raw[0][:])
+            regroup(nc.vector.tensor_copy, w_grouped[:, 1, :, :], w_raw[1][:])
+
+            x_grouped = None
+            if i < ROUNDS:
+                words = x_raw[:].bitcast(F32)
+                xT_ps = work.tile([P, ROUND_PASSES, 2, B], F32, tag="work")
+                for c in range(ROUND_PASSES):
+                    first_word = ((i % X_LOAD_ROUNDS) * ROUND_PASSES + c) * (K_PASS // 2)
+                    for u in range(2):
+                        nc.tensor.transpose(
+                            xT_ps[:, c, u, :],
+                            words[:, first_word + u : first_word + K_PASS // 2 : 2],
+                            ident_f32[:],
+                        )
+                x_grouped = x_grouped_pool.tile([P, ROUND_PASSES * B * PACK], BF16, align_bytes=64)
+                nc.scalar.copy(
+                    out=x_grouped[:].bitcast(F32).rearrange("p (c b u) -> p c b u", c=ROUND_PASSES, u=2),
+                    in_=xT_ps[:].rearrange("p c u b -> p c b u"),
+                )
+            return w_grouped, x_grouped
+
+        def quantise_and_multiply(i, w_grouped, x_grouped):
+            first_pass = (i % ROUNDS) * ROUND_PASSES
+            w_codes = w_mx_pool.tile([P, ROUND_PASSES * H], U32, align_bytes=64)
+            w_scales = w_mx_pool.tile([P, ROUND_PASSES * H], U8, align_bytes=64)
+            nc.vector.quantize_mx(
+                out=w_codes[:].bitcast(FP8X4),
+                scales=w_scales[:],
+                in_=w_grouped[:].rearrange("p c n t -> p (c n t)"),
+            )
+            if x_grouped is not None:
+                x_cols = slice(first_pass * B, (first_pass + ROUND_PASSES) * B)
+                nc.vector.quantize_mx(
+                    out=x_codes[:, x_cols].bitcast(FP8X4), scales=x_scales[:, x_cols], in_=x_grouped[:]
+                )
+            for c in range(ROUND_PASSES):
+                s = first_pass + c
+                x_cols = slice(s * B, (s + 1) * B)
+                if i < ROUNDS:
+                    for m in range(H_TILES):
+                        w_cols = slice(c * H + m * P, c * H + (m + 1) * P)
+                        nc.tensor.matmul_mx(
+                            out=rT[m][:],
+                            lhsT=w_codes[:, w_cols].bitcast(FP8X4),
+                            lhsT_scale=w_scales[:, w_cols],
+                            rhs=x_codes[:, x_cols].bitcast(FP8X4),
+                            rhs_scale=x_scales[:, x_cols],
+                            start=(s == 0),
+                            stop=(s == PASSES - 1),
+                        )
+                else:
+                    w_cols = slice(c * H, (c + 1) * H)
+                    nc.tensor.matmul_mx(
+                        out=cand[:],
+                        lhsT=x_codes[:, x_cols].bitcast(FP8X4),
+                        lhsT_scale=x_scales[:, x_cols],
+                        rhs=w_codes[:, w_cols].bitcast(FP8X4),
+                        rhs_scale=w_scales[:, w_cols],
+                        start=(s == 0),
+                        stop=(s == PASSES - 1),
+                    )
+
+        laid_out = None
+        x_raw = None
+        for i in range(2 * ROUNDS + 1):
+            previous = laid_out
+            if i < 2 * ROUNDS:
+                if i < ROUNDS and i % X_LOAD_ROUNDS == 0:
+                    x_raw = x_raw_pool.tile([B, X_LOAD_ROUNDS * ROUND_K], BF16)
+                    first_k = i * ROUND_K
+                    nc.sync.dma_start(out=x_raw[:], in_=mgn_h[:, first_k : first_k + X_LOAD_ROUNDS * ROUND_K])
+                laid_out = fetch_and_regroup(i, x_raw)
+
+            if i == U_LOAD_ROUND:
+                for gate, u in (("r", U_r), ("h", U_h)):
+                    nc.sync.dma_start(out=u_raw[gate][:], in_=u.rearrange("(t p) n -> p t n", p=P))
+            if i == ROUNDS + 1:
+                for m in range(H_TILES):
+                    nc.scalar.activation(
+                        out=tanh_rT[:, m, :], in_=rT[m][:], func=ACT.Tanh, bias=half_br[:, m : m + 1], scale=0.5
+                    )
+            if i == ROUNDS + 2:
+                nc.vector.scalar_tensor_tensor(
+                    out=g_grouped[:],
+                    in0=tanh_rT[:].rearrange("p t b -> p b t"),
+                    scalar=1.0,
+                    in1=half_hT[:].rearrange("p t b -> p b t"),
+                    op0=ALU.add,
+                    op1=ALU.mult,
+                )
+
+            if i >= 1:
+                quantise_and_multiply(i - 1, previous[0], previous[1])
+
+            if i == U_READY_ROUND:
+                prepare_small_operands()
+            if i == ROUNDS + 2:
+                nc.vector.quantize_mx(
+                    out=g_codes[:].bitcast(FP8X4),
+                    scales=g_scales[:],
+                    in_=g_grouped[:].rearrange("p b t -> p (b t)"),
+                )
+                nc.tensor.matmul_mx(
+                    out=cand[:],
+                    lhsT=g_codes[:].bitcast(FP8X4),
+                    lhsT_scale=g_scales[:],
+                    rhs=u_codes["h"][:].bitcast(FP8X4),
+                    rhs_scale=u_scales["h"][:],
+                    start=False,
+                    stop=False,
+                )
+
+        biased = keep.tile([B, H], F32)
+        nc.vector.tensor_tensor(out=biased[:], in0=cand[:], in1=bh_all[:], op=ALU.add)
+        result = keep.tile([B, H], F32)
+        nc.scalar.activation(out=result[:], in_=biased[:], func=ACT.Tanh)
+        nc.sync.dma_start(out=out, in_=result[:])

@@ -16,16 +16,20 @@ PACK = 4
 K_PASS = P * PACK
 
 B, IN, H = 128, 16384, 512
-PASSES = IN // K_PASS
 H_TILES = H // P
+X_PASSES = IN // K_PASS
+GATE_PASSES = X_PASSES + H // K_PASS
+RESET, CANDIDATE = 0, 1
 
 ROUND_PASSES = 2
-ROUND_K = ROUND_PASSES * K_PASS
-ROUNDS = PASSES // ROUND_PASSES
+ROUNDS = 2 * GATE_PASSES // ROUND_PASSES
+X_ROUNDS = X_PASSES // ROUND_PASSES
 X_LOAD_ROUNDS = 2
-U_LOAD_ROUND = 1
-U_READY_ROUND = 3
+RESET_SUMMED = GATE_PASSES // ROUND_PASSES + 1
 RUN = 4
+
+SLOT_JOINT_H = X_PASSES
+SLOT_G = X_PASSES + 1
 
 FLOPS = 2 * B * H * (2 * IN + 2 * H)
 
@@ -73,81 +77,53 @@ def tile_joint_gru_pa_k_kernel(tc, joint_h, mgn_h, W_r, W_h, U_r, U_h, b_r, b_h,
         rT = [sums.tile([P, B], F32, name="rT%d" % m) for m in range(H_TILES)]
         cand = sums.tile([B, H], F32)
 
-        x_codes = keep.tile([P, PASSES * B], U32, align_bytes=64)
-        x_scales = keep.tile([P, PASSES * B], U8, align_bytes=64)
+        act_codes = keep.tile([P, (X_PASSES + 2) * B], U32, align_bytes=64)
+        act_scales = keep.tile([P, (X_PASSES + 2) * B], U8, align_bytes=64)
 
-        u_raw, u_grouped, u_codes, u_scales = {}, {}, {}, {}
-        for gate in ("r", "h"):
-            u_raw[gate] = keep.tile([P, PACK, H], BF16, name="u_raw_" + gate)
-            u_grouped[gate] = keep.tile([P, H, PACK], BF16, name="u_grouped_" + gate, align_bytes=64)
-            u_codes[gate] = keep.tile([P, H], U32, name="u_codes_" + gate, align_bytes=64)
-            u_scales[gate] = keep.tile([P, H], U8, name="u_scales_" + gate, align_bytes=64)
-        h_grouped = keep.tile([P, B, PACK], BF16, align_bytes=64)
-        h_codes = keep.tile([P, B], U32, align_bytes=64)
-        h_scales = keep.tile([P, B], U8, align_bytes=64)
-        half_hT = keep.tile([P, H_TILES, B], F32)
-        half_br = keep.tile([P, H_TILES], F32)
-        bh_all = keep.tile([P, H], F32)
-        tanh_rT = keep.tile([P, H_TILES, B], F32)
-        g_grouped = keep.tile([P, B, PACK], BF16, align_bytes=64)
-        g_codes = keep.tile([P, B], U32, align_bytes=64)
-        g_scales = keep.tile([P, B], U8, align_bytes=64)
-
-        def prepare_small_operands():
-            hT_ps = work.tile([P, H_TILES, B], BF16, tag="work")
-            for t in range(H_TILES):
-                nc.tensor.transpose(hT_ps[:, t, :], h_sb[:, t * P : (t + 1) * P], ident_bf16[:])
-            brT_ps = work.tile([P, P], BF16, tag="work")
-            nc.tensor.transpose(brT_ps[:], br_rows[:], ident_bf16[:])
-            bh_ps = work.tile([P, H], F32, tag="work")
-            nc.tensor.matmul(bh_ps[:], lhsT=ones[:], rhs=bh_rows[:], start=True, stop=True)
-
-            nc.vector.tensor_copy(out=h_grouped[:], in_=hT_ps[:].rearrange("p t b -> p b t"))
-            nc.scalar.mul(out=half_hT[:], in_=hT_ps[:], mul=0.5)
-            nc.scalar.mul(out=half_br[:], in_=brT_ps[:, 0:H_TILES], mul=0.5)
-            nc.scalar.copy(out=bh_all[:], in_=bh_ps[:])
-            regroup(nc.vector.tensor_copy, u_grouped["r"][:], u_raw["r"][:])
-            regroup(nc.vector.tensor_copy, u_grouped["h"][:], u_raw["h"][:])
-
+        def quantise_activations(first_slot, grouped):
+            cols = slice(first_slot * B, first_slot * B + grouped.shape[1] // PACK)
             nc.vector.quantize_mx(
-                out=h_codes[:].bitcast(FP8X4),
-                scales=h_scales[:],
-                in_=h_grouped[:].rearrange("p b t -> p (b t)"),
+                out=act_codes[:, cols].bitcast(FP8X4), scales=act_scales[:, cols], in_=grouped
             )
-            for gate in ("r", "h"):
-                nc.vector.quantize_mx(
-                    out=u_codes[gate][:].bitcast(FP8X4),
-                    scales=u_scales[gate][:],
-                    in_=u_grouped[gate][:].rearrange("p n t -> p (n t)"),
-                )
-            for m in range(H_TILES):
-                nc.tensor.matmul_mx(
-                    out=rT[m][:],
-                    lhsT=u_codes["r"][:, m * P : (m + 1) * P].bitcast(FP8X4),
-                    lhsT_scale=u_scales["r"][:, m * P : (m + 1) * P],
-                    rhs=h_codes[:].bitcast(FP8X4),
-                    rhs_scale=h_scales[:],
-                    start=False,
-                    stop=False,
-                )
+
+        hT_ps = work.tile([P, H_TILES, B], BF16, tag="work")
+        for t in range(H_TILES):
+            nc.tensor.transpose(hT_ps[:, t, :], h_sb[:, t * P : (t + 1) * P], ident_bf16[:])
+        h_grouped = keep.tile([P, B, PACK], BF16, align_bytes=64)
+        nc.vector.tensor_copy(out=h_grouped[:], in_=hT_ps[:].rearrange("p t b -> p b t"))
+        half_hT = keep.tile([P, H_TILES, B], F32)
+        nc.vector.tensor_scalar_mul(out=half_hT[:], in0=hT_ps[:], scalar1=0.5)
+
+        brT_ps = work.tile([P, P], BF16, tag="work")
+        nc.tensor.transpose(brT_ps[:], br_rows[:], ident_bf16[:])
+        half_br = keep.tile([P, H_TILES], F32)
+        nc.vector.tensor_scalar_mul(out=half_br[:], in0=brT_ps[:, 0:H_TILES], scalar1=0.5)
+
+        bh_ps = work.tile([P, H], F32, tag="work")
+        nc.tensor.matmul(bh_ps[:], lhsT=ones[:], rhs=bh_rows[:], start=True, stop=True)
+        bh_all = keep.tile([P, H], F32)
+        nc.vector.tensor_copy(out=bh_all[:], in_=bh_ps[:])
+
+        quantise_activations(SLOT_JOINT_H, h_grouped[:].rearrange("p b t -> p (b t)"))
+
+        def weight_block(gate, s):
+            if s < X_PASSES:
+                return (W_r, W_h)[gate][s * K_PASS : (s + 1) * K_PASS, :].rearrange("(p t) n -> p t n", p=P)
+            return (U_r, U_h)[gate].rearrange("(t p) n -> p t n", p=P)
 
         def fetch_and_regroup(i, x_raw):
-            weights = W_r if i < ROUNDS else W_h
             w_raw = []
             for c in range(ROUND_PASSES):
-                first_row = (i % ROUNDS) * ROUND_K + c * K_PASS
+                gate, s = divmod(i * ROUND_PASSES + c, GATE_PASSES)
                 w_raw.append(w_raw_pool.tile([P, PACK, H], BF16, name="w_raw%d" % c))
-                nc.sync.dma_start(
-                    out=w_raw[c][:],
-                    in_=weights[first_row : first_row + K_PASS, :].rearrange("(p t) n -> p t n", p=P),
-                )
+                nc.sync.dma_start(out=w_raw[c][:], in_=weight_block(gate, s))
 
             w_grouped = w_grouped_pool.tile([P, ROUND_PASSES, H, PACK], BF16, align_bytes=64)
             regroup(nc.scalar.copy, w_grouped[:, 0, :, :], w_raw[0][:])
             regroup(nc.vector.tensor_copy, w_grouped[:, 1, :, :], w_raw[1][:])
 
             x_grouped = None
-            if i < ROUNDS:
+            if i < X_ROUNDS:
                 words = x_raw[:].bitcast(F32)
                 xT_ps = work.tile([P, ROUND_PASSES, 2, B], F32, tag="work")
                 for c in range(ROUND_PASSES):
@@ -166,7 +142,6 @@ def tile_joint_gru_pa_k_kernel(tc, joint_h, mgn_h, W_r, W_h, U_r, U_h, b_r, b_h,
             return w_grouped, x_grouped
 
         def quantise_and_multiply(i, w_grouped, x_grouped):
-            first_pass = (i % ROUNDS) * ROUND_PASSES
             w_codes = w_mx_pool.tile([P, ROUND_PASSES * H], U32, align_bytes=64)
             w_scales = w_mx_pool.tile([P, ROUND_PASSES * H], U8, align_bytes=64)
             nc.vector.quantize_mx(
@@ -175,57 +150,56 @@ def tile_joint_gru_pa_k_kernel(tc, joint_h, mgn_h, W_r, W_h, U_r, U_h, b_r, b_h,
                 in_=w_grouped[:].rearrange("p c n t -> p (c n t)"),
             )
             if x_grouped is not None:
-                x_cols = slice(first_pass * B, (first_pass + ROUND_PASSES) * B)
-                nc.vector.quantize_mx(
-                    out=x_codes[:, x_cols].bitcast(FP8X4), scales=x_scales[:, x_cols], in_=x_grouped[:]
-                )
+                quantise_activations(i * ROUND_PASSES, x_grouped[:])
+
             for c in range(ROUND_PASSES):
-                s = first_pass + c
-                x_cols = slice(s * B, (s + 1) * B)
-                if i < ROUNDS:
+                gate, s = divmod(i * ROUND_PASSES + c, GATE_PASSES)
+                slot = s if s < X_PASSES else (SLOT_JOINT_H, SLOT_G)[gate]
+                a_cols = slice(slot * B, (slot + 1) * B)
+                if gate == RESET:
                     for m in range(H_TILES):
                         w_cols = slice(c * H + m * P, c * H + (m + 1) * P)
                         nc.tensor.matmul_mx(
                             out=rT[m][:],
                             lhsT=w_codes[:, w_cols].bitcast(FP8X4),
                             lhsT_scale=w_scales[:, w_cols],
-                            rhs=x_codes[:, x_cols].bitcast(FP8X4),
-                            rhs_scale=x_scales[:, x_cols],
+                            rhs=act_codes[:, a_cols].bitcast(FP8X4),
+                            rhs_scale=act_scales[:, a_cols],
                             start=(s == 0),
-                            stop=(s == PASSES - 1),
+                            stop=(s == GATE_PASSES - 1),
                         )
                 else:
                     w_cols = slice(c * H, (c + 1) * H)
                     nc.tensor.matmul_mx(
                         out=cand[:],
-                        lhsT=x_codes[:, x_cols].bitcast(FP8X4),
-                        lhsT_scale=x_scales[:, x_cols],
+                        lhsT=act_codes[:, a_cols].bitcast(FP8X4),
+                        lhsT_scale=act_scales[:, a_cols],
                         rhs=w_codes[:, w_cols].bitcast(FP8X4),
                         rhs_scale=w_scales[:, w_cols],
                         start=(s == 0),
-                        stop=(s == PASSES - 1),
+                        stop=(s == GATE_PASSES - 1),
                     )
+
+        tanh_rT = keep.tile([P, H_TILES, B], F32)
+        g_grouped = keep.tile([P, B, PACK], BF16, align_bytes=64)
 
         laid_out = None
         x_raw = None
-        for i in range(2 * ROUNDS + 1):
+        for i in range(ROUNDS + 1):
             previous = laid_out
-            if i < 2 * ROUNDS:
-                if i < ROUNDS and i % X_LOAD_ROUNDS == 0:
-                    x_raw = x_raw_pool.tile([B, X_LOAD_ROUNDS * ROUND_K], BF16)
-                    first_k = i * ROUND_K
-                    nc.sync.dma_start(out=x_raw[:], in_=mgn_h[:, first_k : first_k + X_LOAD_ROUNDS * ROUND_K])
+            if i < ROUNDS:
+                if i < X_ROUNDS and i % X_LOAD_ROUNDS == 0:
+                    x_raw = x_raw_pool.tile([B, X_LOAD_ROUNDS * ROUND_PASSES * K_PASS], BF16)
+                    first_k = i * ROUND_PASSES * K_PASS
+                    nc.sync.dma_start(out=x_raw[:], in_=mgn_h[:, first_k : first_k + x_raw.shape[1]])
                 laid_out = fetch_and_regroup(i, x_raw)
 
-            if i == U_LOAD_ROUND:
-                for gate, u in (("r", U_r), ("h", U_h)):
-                    nc.sync.dma_start(out=u_raw[gate][:], in_=u.rearrange("(t p) n -> p t n", p=P))
-            if i == ROUNDS + 1:
+            if i == RESET_SUMMED + 1:
                 for m in range(H_TILES):
                     nc.scalar.activation(
                         out=tanh_rT[:, m, :], in_=rT[m][:], func=ACT.Tanh, bias=half_br[:, m : m + 1], scale=0.5
                     )
-            if i == ROUNDS + 2:
+            if i == RESET_SUMMED + 2:
                 nc.vector.scalar_tensor_tensor(
                     out=g_grouped[:],
                     in0=tanh_rT[:].rearrange("p t b -> p b t"),
@@ -238,23 +212,8 @@ def tile_joint_gru_pa_k_kernel(tc, joint_h, mgn_h, W_r, W_h, U_r, U_h, b_r, b_h,
             if i >= 1:
                 quantise_and_multiply(i - 1, previous[0], previous[1])
 
-            if i == U_READY_ROUND:
-                prepare_small_operands()
-            if i == ROUNDS + 2:
-                nc.vector.quantize_mx(
-                    out=g_codes[:].bitcast(FP8X4),
-                    scales=g_scales[:],
-                    in_=g_grouped[:].rearrange("p b t -> p (b t)"),
-                )
-                nc.tensor.matmul_mx(
-                    out=cand[:],
-                    lhsT=g_codes[:].bitcast(FP8X4),
-                    lhsT_scale=g_scales[:],
-                    rhs=u_codes["h"][:].bitcast(FP8X4),
-                    rhs_scale=u_scales["h"][:],
-                    start=False,
-                    stop=False,
-                )
+            if i == RESET_SUMMED + 2:
+                quantise_activations(SLOT_G, g_grouped[:].rearrange("p b t -> p (b t)"))
 
         biased = keep.tile([B, H], F32)
         nc.vector.tensor_tensor(out=biased[:], in0=cand[:], in1=bh_all[:], op=ALU.add)

@@ -26,6 +26,8 @@ ROUNDS = 2 * GATE_PASSES // ROUND_PASSES
 X_ROUNDS = X_PASSES // ROUND_PASSES
 X_LOAD_ROUNDS = 2
 RESET_SUMMED = GATE_PASSES // ROUND_PASSES + 1
+SMALL_LOADED = 4
+SMALL_LAID_OUT = 8
 RUN = 4
 
 SLOT_JOINT_H = X_PASSES
@@ -62,13 +64,10 @@ def tile_joint_gru_pa_k_kernel(tc, joint_h, mgn_h, W_r, W_h, U_r, U_h, b_r, b_h,
         nc.vector.memset(ones[:], 1.0)
 
         h_sb = keep.tile([B, H], BF16)
-        nc.scalar.dma_start(out=h_sb[:], in_=joint_h)
         br_rows = keep.tile([P, P], BF16)
         nc.vector.memset(br_rows[:], 0.0)
-        nc.scalar.dma_start(out=br_rows[0:H_TILES, :], in_=b_r.rearrange("(t p) -> t p", p=P))
         bh_rows = keep.tile([P, H], BF16)
         nc.vector.memset(bh_rows[:], 0.0)
-        nc.scalar.dma_start(out=bh_rows[0:1, :], in_=b_h.unsqueeze(0))
 
         warm = keep.tile([P, 1], F32)
         nc.vector.memset(warm[:], 0.0)
@@ -86,38 +85,49 @@ def tile_joint_gru_pa_k_kernel(tc, joint_h, mgn_h, W_r, W_h, U_r, U_h, b_r, b_h,
                 out=act_codes[:, cols].bitcast(FP8X4), scales=act_scales[:, cols], in_=grouped
             )
 
-        hT_ps = work.tile([P, H_TILES, B], BF16, tag="work")
-        for t in range(H_TILES):
-            nc.tensor.transpose(hT_ps[:, t, :], h_sb[:, t * P : (t + 1) * P], ident_bf16[:])
         h_grouped = keep.tile([P, B, PACK], BF16, align_bytes=64)
-        nc.vector.tensor_copy(out=h_grouped[:], in_=hT_ps[:].rearrange("p t b -> p b t"))
         half_hT = keep.tile([P, H_TILES, B], F32)
-        nc.vector.tensor_scalar_mul(out=half_hT[:], in0=hT_ps[:], scalar1=0.5)
-
-        brT_ps = work.tile([P, P], BF16, tag="work")
-        nc.tensor.transpose(brT_ps[:], br_rows[:], ident_bf16[:])
         half_br = keep.tile([P, H_TILES], F32)
-        nc.vector.tensor_scalar_mul(out=half_br[:], in0=brT_ps[:, 0:H_TILES], scalar1=0.5)
-
-        bh_ps = work.tile([P, H], F32, tag="work")
-        nc.tensor.matmul(bh_ps[:], lhsT=ones[:], rhs=bh_rows[:], start=True, stop=True)
         bh_all = keep.tile([P, H], F32)
-        nc.vector.tensor_copy(out=bh_all[:], in_=bh_ps[:])
 
-        quantise_activations(SLOT_JOINT_H, h_grouped[:].rearrange("p b t -> p (b t)"))
+        def load_small_operands():
+            nc.sync.dma_start(out=h_sb[:], in_=joint_h)
+            nc.sync.dma_start(out=br_rows[0:H_TILES, :], in_=b_r.rearrange("(t p) -> t p", p=P))
+            nc.sync.dma_start(out=bh_rows[0:1, :], in_=b_h.unsqueeze(0))
+
+        def lay_out_small_operands():
+            hT_ps = work.tile([P, H_TILES, B], BF16, tag="work")
+            for t in range(H_TILES):
+                nc.tensor.transpose(hT_ps[:, t, :], h_sb[:, t * P : (t + 1) * P], ident_bf16[:])
+            nc.vector.tensor_copy(out=h_grouped[:], in_=hT_ps[:].rearrange("p t b -> p b t"))
+            nc.vector.tensor_scalar_mul(out=half_hT[:], in0=hT_ps[:], scalar1=0.5)
+
+            brT_ps = work.tile([P, P], BF16, tag="work")
+            nc.tensor.transpose(brT_ps[:], br_rows[:], ident_bf16[:])
+            nc.vector.tensor_scalar_mul(out=half_br[:], in0=brT_ps[:, 0:H_TILES], scalar1=0.5)
+
+            bh_ps = work.tile([P, H], F32, tag="work")
+            nc.tensor.matmul(bh_ps[:], lhsT=ones[:], rhs=bh_rows[:], start=True, stop=True)
+            nc.vector.tensor_copy(out=bh_all[:], in_=bh_ps[:])
 
         def weight_block(gate, s):
             if s < X_PASSES:
                 return (W_r, W_h)[gate][s * K_PASS : (s + 1) * K_PASS, :].rearrange("(p t) n -> p t n", p=P)
             return (U_r, U_h)[gate].rearrange("(t p) n -> p t n", p=P)
 
-        def fetch_and_regroup(i, x_raw):
+        def load_round(i, x_raw):
             w_raw = []
             for c in range(ROUND_PASSES):
                 gate, s = divmod(i * ROUND_PASSES + c, GATE_PASSES)
                 w_raw.append(w_raw_pool.tile([P, PACK, H], BF16, name="w_raw%d" % c))
                 nc.sync.dma_start(out=w_raw[c][:], in_=weight_block(gate, s))
+            if i < X_ROUNDS and i % X_LOAD_ROUNDS == 0:
+                x_raw = x_raw_pool.tile([B, X_LOAD_ROUNDS * ROUND_PASSES * K_PASS], BF16)
+                first_k = i * ROUND_PASSES * K_PASS
+                nc.sync.dma_start(out=x_raw[:], in_=mgn_h[:, first_k : first_k + x_raw.shape[1]])
+            return w_raw, x_raw
 
+        def regroup_round(i, w_raw, x_raw):
             w_grouped = w_grouped_pool.tile([P, ROUND_PASSES, H, PACK], BF16, align_bytes=64)
             regroup(nc.scalar.copy, w_grouped[:, 0, :, :], w_raw[0][:])
             regroup(nc.vector.tensor_copy, w_grouped[:, 1, :, :], w_raw[1][:])
@@ -188,11 +198,10 @@ def tile_joint_gru_pa_k_kernel(tc, joint_h, mgn_h, W_r, W_h, U_r, U_h, b_r, b_h,
         for i in range(ROUNDS + 1):
             previous = laid_out
             if i < ROUNDS:
-                if i < X_ROUNDS and i % X_LOAD_ROUNDS == 0:
-                    x_raw = x_raw_pool.tile([B, X_LOAD_ROUNDS * ROUND_PASSES * K_PASS], BF16)
-                    first_k = i * ROUND_PASSES * K_PASS
-                    nc.sync.dma_start(out=x_raw[:], in_=mgn_h[:, first_k : first_k + x_raw.shape[1]])
-                laid_out = fetch_and_regroup(i, x_raw)
+                w_raw, x_raw = load_round(i, x_raw)
+                if i == SMALL_LOADED:
+                    load_small_operands()
+                laid_out = regroup_round(i, w_raw, x_raw)
 
             if i == RESET_SUMMED + 1:
                 for m in range(H_TILES):
@@ -211,6 +220,11 @@ def tile_joint_gru_pa_k_kernel(tc, joint_h, mgn_h, W_r, W_h, U_r, U_h, b_r, b_h,
 
             if i >= 1:
                 quantise_and_multiply(i - 1, previous[0], previous[1])
+
+            if i == SMALL_LAID_OUT:
+                lay_out_small_operands()
+            if i == SMALL_LAID_OUT + 1:
+                quantise_activations(SLOT_JOINT_H, h_grouped[:].rearrange("p b t -> p (b t)"))
 
             if i == RESET_SUMMED + 2:
                 quantise_activations(SLOT_G, g_grouped[:].rearrange("p b t -> p (b t)"))

@@ -27,7 +27,7 @@ X_ROUNDS = X_PASSES // ROUND_PASSES
 X_LOAD_ROUNDS = 2
 RESET_SUMMED = GATE_PASSES // ROUND_PASSES + 1
 SMALL_LOADED = 4
-SMALL_LAID_OUT = 8
+SMALL_LAID_OUT = (7, 9, 11)
 RUN = 4
 
 SLOT_JOINT_H = X_PASSES
@@ -74,7 +74,6 @@ def tile_joint_gru_pa_k_kernel(tc, joint_h, mgn_h, W_r, W_h, U_r, U_h, b_r, b_h,
         nc.scalar.activation(out=warm[:], in_=warm[:], func=ACT.Tanh)
 
         rT = [sums.tile([P, B], F32, name="rT%d" % m) for m in range(H_TILES)]
-        cand = sums.tile([B, H], F32)
 
         act_codes = keep.tile([P, (X_PASSES + 2) * B], U32, align_bytes=64)
         act_scales = keep.tile([P, (X_PASSES + 2) * B], U8, align_bytes=64)
@@ -95,55 +94,62 @@ def tile_joint_gru_pa_k_kernel(tc, joint_h, mgn_h, W_r, W_h, U_r, U_h, b_r, b_h,
             nc.sync.dma_start(out=br_rows[0:H_TILES, :], in_=b_r.rearrange("(t p) -> t p", p=P))
             nc.sync.dma_start(out=bh_rows[0:1, :], in_=b_h.unsqueeze(0))
 
-        def lay_out_small_operands():
-            hT_ps = work.tile([P, H_TILES, B], BF16, tag="work")
+        def lay_out_joint_h():
+            hT_ps = sums.tile([P, H_TILES, B], BF16, tag="fifth")
             for t in range(H_TILES):
                 nc.tensor.transpose(hT_ps[:, t, :], h_sb[:, t * P : (t + 1) * P], ident_bf16[:])
-            nc.vector.tensor_copy(out=h_grouped[:], in_=hT_ps[:].rearrange("p t b -> p b t"))
-            nc.vector.tensor_scalar_mul(out=half_hT[:], in0=hT_ps[:], scalar1=0.5)
+            nc.scalar.copy(out=h_grouped[:], in_=hT_ps[:].rearrange("p t b -> p b t"))
+            nc.scalar.mul(half_hT[:], hT_ps[:], 0.5)
 
-            brT_ps = work.tile([P, P], BF16, tag="work")
+        def lay_out_b_r():
+            brT_ps = sums.tile([P, P], BF16, tag="fifth")
             nc.tensor.transpose(brT_ps[:], br_rows[:], ident_bf16[:])
-            nc.vector.tensor_scalar_mul(out=half_br[:], in0=brT_ps[:, 0:H_TILES], scalar1=0.5)
+            nc.scalar.mul(half_br[:], brT_ps[:, 0:H_TILES], 0.5)
 
-            bh_ps = work.tile([P, H], F32, tag="work")
+        def lay_out_b_h():
+            bh_ps = sums.tile([P, H], F32, tag="fifth")
             nc.tensor.matmul(bh_ps[:], lhsT=ones[:], rhs=bh_rows[:], start=True, stop=True)
-            nc.vector.tensor_copy(out=bh_all[:], in_=bh_ps[:])
+            nc.scalar.copy(out=bh_all[:], in_=bh_ps[:])
 
         def weight_block(gate, s):
             if s < X_PASSES:
                 return (W_r, W_h)[gate][s * K_PASS : (s + 1) * K_PASS, :].rearrange("(p t) n -> p t n", p=P)
             return (U_r, U_h)[gate].rearrange("(t p) n -> p t n", p=P)
 
-        def load_round(i, x_raw):
+        def load_x(i):
+            x_raw = x_raw_pool.tile([B, X_LOAD_ROUNDS * ROUND_PASSES * K_PASS], BF16)
+            first_k = i * ROUND_PASSES * K_PASS
+            nc.sync.dma_start(out=x_raw[:], in_=mgn_h[:, first_k : first_k + x_raw.shape[1]])
+            return x_raw
+
+        def load_weights(i):
             w_raw = []
             for c in range(ROUND_PASSES):
                 gate, s = divmod(i * ROUND_PASSES + c, GATE_PASSES)
                 w_raw.append(w_raw_pool.tile([P, PACK, H], BF16, name="w_raw%d" % c))
                 nc.sync.dma_start(out=w_raw[c][:], in_=weight_block(gate, s))
-            if i < X_ROUNDS and i % X_LOAD_ROUNDS == 0:
-                x_raw = x_raw_pool.tile([B, X_LOAD_ROUNDS * ROUND_PASSES * K_PASS], BF16)
-                first_k = i * ROUND_PASSES * K_PASS
-                nc.sync.dma_start(out=x_raw[:], in_=mgn_h[:, first_k : first_k + x_raw.shape[1]])
-            return w_raw, x_raw
+            return w_raw
 
-        def regroup_round(i, w_raw, x_raw):
+        def transpose_x(i, x_raw):
+            words = x_raw[:].bitcast(F32)
+            xT_ps = work.tile([P, ROUND_PASSES, 2, B], F32, tag="work")
+            for c in range(ROUND_PASSES):
+                first_word = ((i % X_LOAD_ROUNDS) * ROUND_PASSES + c) * (K_PASS // 2)
+                for u in range(2):
+                    nc.tensor.transpose(
+                        xT_ps[:, c, u, :],
+                        words[:, first_word + u : first_word + K_PASS // 2 : 2],
+                        ident_f32[:],
+                    )
+            return xT_ps
+
+        def regroup_round(w_raw, xT_ps):
             w_grouped = w_grouped_pool.tile([P, ROUND_PASSES, H, PACK], BF16, align_bytes=64)
             regroup(nc.scalar.copy, w_grouped[:, 0, :, :], w_raw[0][:])
             regroup(nc.vector.tensor_copy, w_grouped[:, 1, :, :], w_raw[1][:])
 
             x_grouped = None
-            if i < X_ROUNDS:
-                words = x_raw[:].bitcast(F32)
-                xT_ps = work.tile([P, ROUND_PASSES, 2, B], F32, tag="work")
-                for c in range(ROUND_PASSES):
-                    first_word = ((i % X_LOAD_ROUNDS) * ROUND_PASSES + c) * (K_PASS // 2)
-                    for u in range(2):
-                        nc.tensor.transpose(
-                            xT_ps[:, c, u, :],
-                            words[:, first_word + u : first_word + K_PASS // 2 : 2],
-                            ident_f32[:],
-                        )
+            if xT_ps is not None:
                 x_grouped = x_grouped_pool.tile([P, ROUND_PASSES * B * PACK], BF16, align_bytes=64)
                 nc.scalar.copy(
                     out=x_grouped[:].bitcast(F32).rearrange("p (c b u) -> p c b u", c=ROUND_PASSES, u=2),
@@ -151,7 +157,7 @@ def tile_joint_gru_pa_k_kernel(tc, joint_h, mgn_h, W_r, W_h, U_r, U_h, b_r, b_h,
                 )
             return w_grouped, x_grouped
 
-        def quantise_and_multiply(i, w_grouped, x_grouped):
+        def quantise_and_multiply(i, w_grouped, x_grouped, cand):
             w_codes = w_mx_pool.tile([P, ROUND_PASSES * H], U32, align_bytes=64)
             w_scales = w_mx_pool.tile([P, ROUND_PASSES * H], U8, align_bytes=64)
             nc.vector.quantize_mx(
@@ -193,15 +199,29 @@ def tile_joint_gru_pa_k_kernel(tc, joint_h, mgn_h, W_r, W_h, U_r, U_h, b_r, b_h,
         tanh_rT = keep.tile([P, H_TILES, B], F32)
         g_grouped = keep.tile([P, B, PACK], BF16, align_bytes=64)
 
+        small_steps = dict(zip(SMALL_LAID_OUT, (lay_out_joint_h, lay_out_b_r, lay_out_b_h)))
         laid_out = None
         x_raw = None
+        xT_next = None
+        cand = None
         for i in range(ROUNDS + 1):
             previous = laid_out
             if i < ROUNDS:
-                w_raw, x_raw = load_round(i, x_raw)
+                w_raw = load_weights(i)
+                if i == 0:
+                    x_raw = load_x(0)
+                    xT_next = transpose_x(0, x_raw)
+                if i + 1 < X_ROUNDS and (i + 1) % X_LOAD_ROUNDS == 0:
+                    x_raw = load_x(i + 1)
                 if i == SMALL_LOADED:
                     load_small_operands()
-                laid_out = regroup_round(i, w_raw, x_raw)
+                xT_ps = xT_next
+                xT_next = transpose_x(i + 1, x_raw) if i + 1 < X_ROUNDS else None
+                laid_out = regroup_round(w_raw, xT_ps)
+                if i in small_steps:
+                    small_steps[i]()
+                if i == RESET_SUMMED - 1:
+                    cand = sums.tile([B, H], F32, tag="fifth")
 
             if i == RESET_SUMMED + 1:
                 for m in range(H_TILES):
@@ -219,11 +239,9 @@ def tile_joint_gru_pa_k_kernel(tc, joint_h, mgn_h, W_r, W_h, U_r, U_h, b_r, b_h,
                 )
 
             if i >= 1:
-                quantise_and_multiply(i - 1, previous[0], previous[1])
+                quantise_and_multiply(i - 1, previous[0], previous[1], cand)
 
-            if i == SMALL_LAID_OUT:
-                lay_out_small_operands()
-            if i == SMALL_LAID_OUT + 1:
+            if i == SMALL_LAID_OUT[0] + 1:
                 quantise_activations(SLOT_JOINT_H, h_grouped[:].rearrange("p b t -> p (b t)"))
 
             if i == RESET_SUMMED + 2:

@@ -28,6 +28,7 @@ X_LOAD_ROUNDS = 2
 RESET_SUMMED = GATE_PASSES // ROUND_PASSES + 1
 SMALL_LOADED = 4
 SMALL_LAID_OUT = (7, 9, 11)
+VECTOR_COLS = 352
 RUN = 4
 
 SLOT_JOINT_H = X_PASSES
@@ -157,18 +158,23 @@ def tile_joint_gru_pa_k_kernel(tc, joint_h, mgn_h, W_r, W_h, U_r, U_h, b_r, b_h,
                 )
             return w_grouped, x_grouped
 
+        def quantise_weights(w_codes, w_scales, w_grouped, cols):
+            nc.vector.quantize_mx(
+                out=w_codes[:, cols].bitcast(FP8X4),
+                scales=w_scales[:, cols],
+                in_=w_grouped[:].rearrange("p c n t -> p (c n t)")[:, cols.start * PACK : cols.stop * PACK],
+            )
+
         def quantise_and_multiply(i, w_grouped, x_grouped, cand):
             w_codes = w_mx_pool.tile([P, ROUND_PASSES * H], U32, align_bytes=64)
             w_scales = w_mx_pool.tile([P, ROUND_PASSES * H], U8, align_bytes=64)
-            nc.vector.quantize_mx(
-                out=w_codes[:].bitcast(FP8X4),
-                scales=w_scales[:],
-                in_=w_grouped[:].rearrange("p c n t -> p (c n t)"),
-            )
+            quantise_weights(w_codes, w_scales, w_grouped, slice(0, ROUND_PASSES * H))
             if x_grouped is not None:
                 quantise_activations(i * ROUND_PASSES, x_grouped[:])
+            multiply(i, range(ROUND_PASSES), w_codes, w_scales, cand)
 
-            for c in range(ROUND_PASSES):
+        def multiply(i, passes, w_codes, w_scales, cand):
+            for c in passes:
                 gate, s = divmod(i * ROUND_PASSES + c, GATE_PASSES)
                 slot = s if s < X_PASSES else (SLOT_JOINT_H, SLOT_G)[gate]
                 a_cols = slice(slot * B, (slot + 1) * B)
@@ -196,6 +202,20 @@ def tile_joint_gru_pa_k_kernel(tc, joint_h, mgn_h, W_r, W_h, U_r, U_h, b_r, b_h,
                         stop=(s == GATE_PASSES - 1),
                     )
 
+        def last_round(w_raw, cand):
+            i = ROUNDS - 1
+            w_grouped = w_grouped_pool.tile([P, ROUND_PASSES, H, PACK], BF16, align_bytes=64)
+            w_codes = w_mx_pool.tile([P, ROUND_PASSES * H], U32, align_bytes=64)
+            w_scales = w_mx_pool.tile([P, ROUND_PASSES * H], U8, align_bytes=64)
+            for c in range(ROUND_PASSES):
+                regroup(nc.scalar.copy, w_grouped[:, c, VECTOR_COLS:, :], w_raw[c][:, :, VECTOR_COLS:])
+                for cols in (slice(0, H // 2), slice(H // 2, VECTOR_COLS)):
+                    regroup(nc.vector.tensor_copy, w_grouped[:, c, cols, :], w_raw[c][:, :, cols])
+                for half in range(2):
+                    first = c * H + half * (H // 2)
+                    quantise_weights(w_codes, w_scales, w_grouped, slice(first, first + H // 2))
+                multiply(i, [c], w_codes, w_scales, cand)
+
         tanh_rT = keep.tile([P, H_TILES, B], F32)
         g_grouped = keep.tile([P, B, PACK], BF16, align_bytes=64)
 
@@ -204,24 +224,24 @@ def tile_joint_gru_pa_k_kernel(tc, joint_h, mgn_h, W_r, W_h, U_r, U_h, b_r, b_h,
         x_raw = None
         xT_next = None
         cand = None
-        for i in range(ROUNDS + 1):
+        for i in range(ROUNDS):
             previous = laid_out
-            if i < ROUNDS:
-                w_raw = load_weights(i)
-                if i == 0:
-                    x_raw = load_x(0)
-                    xT_next = transpose_x(0, x_raw)
-                if i + 1 < X_ROUNDS and (i + 1) % X_LOAD_ROUNDS == 0:
-                    x_raw = load_x(i + 1)
-                if i == SMALL_LOADED:
-                    load_small_operands()
-                xT_ps = xT_next
-                xT_next = transpose_x(i + 1, x_raw) if i + 1 < X_ROUNDS else None
+            w_raw = load_weights(i)
+            if i == 0:
+                x_raw = load_x(0)
+                xT_next = transpose_x(0, x_raw)
+            if i + 1 < X_ROUNDS and (i + 1) % X_LOAD_ROUNDS == 0:
+                x_raw = load_x(i + 1)
+            if i == SMALL_LOADED:
+                load_small_operands()
+            xT_ps = xT_next
+            xT_next = transpose_x(i + 1, x_raw) if i + 1 < X_ROUNDS else None
+            if i < ROUNDS - 1:
                 laid_out = regroup_round(w_raw, xT_ps)
-                if i in small_steps:
-                    small_steps[i]()
-                if i == RESET_SUMMED - 1:
-                    cand = sums.tile([B, H], F32, tag="fifth")
+            if i in small_steps:
+                small_steps[i]()
+            if i == RESET_SUMMED - 1:
+                cand = sums.tile([B, H], F32, tag="fifth")
 
             if i == RESET_SUMMED + 1:
                 for m in range(H_TILES):
@@ -247,8 +267,12 @@ def tile_joint_gru_pa_k_kernel(tc, joint_h, mgn_h, W_r, W_h, U_r, U_h, b_r, b_h,
             if i == RESET_SUMMED + 2:
                 quantise_activations(SLOT_G, g_grouped[:].rearrange("p b t -> p (b t)"))
 
-        biased = keep.tile([B, H], F32)
-        nc.vector.tensor_tensor(out=biased[:], in0=cand[:], in1=bh_all[:], op=ALU.add)
-        result = keep.tile([B, H], F32)
-        nc.scalar.activation(out=result[:], in_=biased[:], func=ACT.Tanh)
-        nc.sync.dma_start(out=out, in_=result[:])
+        last_round(w_raw, cand)
+
+        for half in range(2):
+            cols = slice(half * (H // 2), (half + 1) * (H // 2))
+            biased = keep.tile([B, H // 2], F32, name="biased%d" % half)
+            nc.vector.tensor_tensor(out=biased[:], in0=cand[:, cols], in1=bh_all[:, cols], op=ALU.add)
+            result = keep.tile([B, H // 2], F32, name="result%d" % half)
+            nc.scalar.activation(out=result[:], in_=biased[:], func=ACT.Tanh)
+            nc.sync.dma_start(out=out[:, cols], in_=result[:])

@@ -21,13 +21,22 @@ X_PASSES = IN // K_PASS
 GATE_PASSES = X_PASSES + H // K_PASS
 RESET, CANDIDATE = 0, 1
 
+RESET_LEAD = 8
+STREAM = (
+    [(RESET, s) for s in range(RESET_LEAD)]
+    + [(gate, s - gate * RESET_LEAD) for s in range(RESET_LEAD, GATE_PASSES) for gate in (RESET, CANDIDATE)]
+    + [(CANDIDATE, s) for s in range(GATE_PASSES - RESET_LEAD, GATE_PASSES)]
+)
+
 ROUND_PASSES = 2
 ROUNDS = 2 * GATE_PASSES // ROUND_PASSES
-X_ROUNDS = X_PASSES // ROUND_PASSES
-X_LOAD_ROUNDS = 2
-RESET_SUMMED = GATE_PASSES // ROUND_PASSES + 1
-SMALL_LOADED = 4
-SMALL_LAID_OUT = (7, 9, 11)
+X_PAIR = 2
+X_LOAD_PAIRS = 2
+X_PAIR_OF_ROUND = {STREAM.index((RESET, m * X_PAIR)) // ROUND_PASSES: m for m in range(X_PASSES // X_PAIR)}
+RESET_SUMMED = STREAM.index((RESET, GATE_PASSES - 1)) // ROUND_PASSES + 1
+SMALL_LOADED = 6
+SMALL_LAID_OUT = (10, 12, 14)
+LEAD_IN = 4
 VECTOR_COLS = 352
 RUN = 4
 
@@ -75,6 +84,7 @@ def tile_joint_gru_pa_k_kernel(tc, joint_h, mgn_h, W_r, W_h, U_r, U_h, b_r, b_h,
         nc.scalar.activation(out=warm[:], in_=warm[:], func=ACT.Tanh)
 
         rT = [sums.tile([P, B], F32, name="rT%d" % m) for m in range(H_TILES)]
+        cand = sums.tile([B, H], F32)
 
         act_codes = keep.tile([P, (X_PASSES + 2) * B], U32, align_bytes=64)
         act_scales = keep.tile([P, (X_PASSES + 2) * B], U8, align_bytes=64)
@@ -96,19 +106,19 @@ def tile_joint_gru_pa_k_kernel(tc, joint_h, mgn_h, W_r, W_h, U_r, U_h, b_r, b_h,
             nc.sync.dma_start(out=bh_rows[0:1, :], in_=b_h.unsqueeze(0))
 
         def lay_out_joint_h():
-            hT_ps = sums.tile([P, H_TILES, B], BF16, tag="fifth")
+            hT_ps = work.tile([P, H_TILES, B], BF16, tag="work")
             for t in range(H_TILES):
                 nc.tensor.transpose(hT_ps[:, t, :], h_sb[:, t * P : (t + 1) * P], ident_bf16[:])
             nc.scalar.copy(out=h_grouped[:], in_=hT_ps[:].rearrange("p t b -> p b t"))
             nc.scalar.mul(half_hT[:], hT_ps[:], 0.5)
 
         def lay_out_b_r():
-            brT_ps = sums.tile([P, P], BF16, tag="fifth")
+            brT_ps = work.tile([P, P], BF16, tag="work")
             nc.tensor.transpose(brT_ps[:], br_rows[:], ident_bf16[:])
             nc.scalar.mul(half_br[:], brT_ps[:, 0:H_TILES], 0.5)
 
         def lay_out_b_h():
-            bh_ps = sums.tile([P, H], F32, tag="fifth")
+            bh_ps = work.tile([P, H], F32, tag="work")
             nc.tensor.matmul(bh_ps[:], lhsT=ones[:], rhs=bh_rows[:], start=True, stop=True)
             nc.scalar.copy(out=bh_all[:], in_=bh_ps[:])
 
@@ -117,25 +127,25 @@ def tile_joint_gru_pa_k_kernel(tc, joint_h, mgn_h, W_r, W_h, U_r, U_h, b_r, b_h,
                 return (W_r, W_h)[gate][s * K_PASS : (s + 1) * K_PASS, :].rearrange("(p t) n -> p t n", p=P)
             return (U_r, U_h)[gate].rearrange("(t p) n -> p t n", p=P)
 
-        def load_x(i):
-            x_raw = x_raw_pool.tile([B, X_LOAD_ROUNDS * ROUND_PASSES * K_PASS], BF16)
-            first_k = i * ROUND_PASSES * K_PASS
+        def load_x(m):
+            x_raw = x_raw_pool.tile([B, X_LOAD_PAIRS * X_PAIR * K_PASS], BF16)
+            first_k = m * X_PAIR * K_PASS
             nc.sync.dma_start(out=x_raw[:], in_=mgn_h[:, first_k : first_k + x_raw.shape[1]])
             return x_raw
 
         def load_weights(i):
             w_raw = []
             for c in range(ROUND_PASSES):
-                gate, s = divmod(i * ROUND_PASSES + c, GATE_PASSES)
+                gate, s = STREAM[i * ROUND_PASSES + c]
                 w_raw.append(w_raw_pool.tile([P, PACK, H], BF16, name="w_raw%d" % c))
                 nc.sync.dma_start(out=w_raw[c][:], in_=weight_block(gate, s))
             return w_raw
 
-        def transpose_x(i, x_raw):
+        def transpose_x(m, x_raw):
             words = x_raw[:].bitcast(F32)
-            xT_ps = work.tile([P, ROUND_PASSES, 2, B], F32, tag="work")
-            for c in range(ROUND_PASSES):
-                first_word = ((i % X_LOAD_ROUNDS) * ROUND_PASSES + c) * (K_PASS // 2)
+            xT_ps = work.tile([P, X_PAIR, 2, B], F32, tag="work")
+            for c in range(X_PAIR):
+                first_word = ((m % X_LOAD_PAIRS) * X_PAIR + c) * (K_PASS // 2)
                 for u in range(2):
                     nc.tensor.transpose(
                         xT_ps[:, c, u, :],
@@ -151,9 +161,9 @@ def tile_joint_gru_pa_k_kernel(tc, joint_h, mgn_h, W_r, W_h, U_r, U_h, b_r, b_h,
 
             x_grouped = None
             if xT_ps is not None:
-                x_grouped = x_grouped_pool.tile([P, ROUND_PASSES * B * PACK], BF16, align_bytes=64)
+                x_grouped = x_grouped_pool.tile([P, X_PAIR * B * PACK], BF16, align_bytes=64)
                 nc.scalar.copy(
-                    out=x_grouped[:].bitcast(F32).rearrange("p (c b u) -> p c b u", c=ROUND_PASSES, u=2),
+                    out=x_grouped[:].bitcast(F32).rearrange("p (c b u) -> p c b u", c=X_PAIR, u=2),
                     in_=xT_ps[:].rearrange("p c u b -> p c b u"),
                 )
             return w_grouped, x_grouped
@@ -165,17 +175,19 @@ def tile_joint_gru_pa_k_kernel(tc, joint_h, mgn_h, W_r, W_h, U_r, U_h, b_r, b_h,
                 in_=w_grouped[:].rearrange("p c n t -> p (c n t)")[:, cols.start * PACK : cols.stop * PACK],
             )
 
-        def quantise_and_multiply(i, w_grouped, x_grouped, cand):
+        def quantise_and_multiply(i, w_grouped, x_grouped):
             w_codes = w_mx_pool.tile([P, ROUND_PASSES * H], U32, align_bytes=64)
             w_scales = w_mx_pool.tile([P, ROUND_PASSES * H], U8, align_bytes=64)
-            quantise_weights(w_codes, w_scales, w_grouped, slice(0, ROUND_PASSES * H))
+            width = H if i < LEAD_IN else ROUND_PASSES * H
+            for first in range(0, ROUND_PASSES * H, width):
+                quantise_weights(w_codes, w_scales, w_grouped, slice(first, first + width))
             if x_grouped is not None:
-                quantise_activations(i * ROUND_PASSES, x_grouped[:])
-            multiply(i, range(ROUND_PASSES), w_codes, w_scales, cand)
+                quantise_activations(X_PAIR_OF_ROUND[i] * X_PAIR, x_grouped[:])
+            multiply(i, range(ROUND_PASSES), w_codes, w_scales)
 
-        def multiply(i, passes, w_codes, w_scales, cand):
+        def multiply(i, passes, w_codes, w_scales):
             for c in passes:
-                gate, s = divmod(i * ROUND_PASSES + c, GATE_PASSES)
+                gate, s = STREAM[i * ROUND_PASSES + c]
                 slot = s if s < X_PASSES else (SLOT_JOINT_H, SLOT_G)[gate]
                 a_cols = slice(slot * B, (slot + 1) * B)
                 if gate == RESET:
@@ -202,7 +214,7 @@ def tile_joint_gru_pa_k_kernel(tc, joint_h, mgn_h, W_r, W_h, U_r, U_h, b_r, b_h,
                         stop=(s == GATE_PASSES - 1),
                     )
 
-        def last_round(w_raw, cand):
+        def last_round(w_raw):
             i = ROUNDS - 1
             w_grouped = w_grouped_pool.tile([P, ROUND_PASSES, H, PACK], BF16, align_bytes=64)
             w_codes = w_mx_pool.tile([P, ROUND_PASSES * H], U32, align_bytes=64)
@@ -214,7 +226,7 @@ def tile_joint_gru_pa_k_kernel(tc, joint_h, mgn_h, W_r, W_h, U_r, U_h, b_r, b_h,
                 for half in range(2):
                     first = c * H + half * (H // 2)
                     quantise_weights(w_codes, w_scales, w_grouped, slice(first, first + H // 2))
-                multiply(i, [c], w_codes, w_scales, cand)
+                multiply(i, [c], w_codes, w_scales)
 
         tanh_rT = keep.tile([P, H_TILES, B], F32)
         g_grouped = keep.tile([P, B, PACK], BF16, align_bytes=64)
@@ -223,25 +235,25 @@ def tile_joint_gru_pa_k_kernel(tc, joint_h, mgn_h, W_r, W_h, U_r, U_h, b_r, b_h,
         laid_out = None
         x_raw = None
         xT_next = None
-        cand = None
         for i in range(ROUNDS):
             previous = laid_out
             w_raw = load_weights(i)
             if i == 0:
                 x_raw = load_x(0)
                 xT_next = transpose_x(0, x_raw)
-            if i + 1 < X_ROUNDS and (i + 1) % X_LOAD_ROUNDS == 0:
-                x_raw = load_x(i + 1)
+            next_pair = X_PAIR_OF_ROUND.get(i + 1)
+            if next_pair is not None and next_pair % X_LOAD_PAIRS == 0:
+                x_raw = load_x(next_pair)
             if i == SMALL_LOADED:
                 load_small_operands()
+            if 1 <= i <= LEAD_IN:
+                quantise_and_multiply(i - 1, previous[0], previous[1])
             xT_ps = xT_next
-            xT_next = transpose_x(i + 1, x_raw) if i + 1 < X_ROUNDS else None
+            xT_next = None if next_pair is None else transpose_x(next_pair, x_raw)
             if i < ROUNDS - 1:
                 laid_out = regroup_round(w_raw, xT_ps)
             if i in small_steps:
                 small_steps[i]()
-            if i == RESET_SUMMED - 1:
-                cand = sums.tile([B, H], F32, tag="fifth")
 
             if i == RESET_SUMMED + 1:
                 for m in range(H_TILES):
@@ -258,8 +270,8 @@ def tile_joint_gru_pa_k_kernel(tc, joint_h, mgn_h, W_r, W_h, U_r, U_h, b_r, b_h,
                     op1=ALU.mult,
                 )
 
-            if i >= 1:
-                quantise_and_multiply(i - 1, previous[0], previous[1], cand)
+            if i > LEAD_IN:
+                quantise_and_multiply(i - 1, previous[0], previous[1])
 
             if i == SMALL_LAID_OUT[0] + 1:
                 quantise_activations(SLOT_JOINT_H, h_grouped[:].rearrange("p b t -> p (b t)"))
@@ -267,7 +279,7 @@ def tile_joint_gru_pa_k_kernel(tc, joint_h, mgn_h, W_r, W_h, U_r, U_h, b_r, b_h,
             if i == RESET_SUMMED + 2:
                 quantise_activations(SLOT_G, g_grouped[:].rearrange("p b t -> p (b t)"))
 
-        last_round(w_raw, cand)
+        last_round(w_raw)
 
         for half in range(2):
             cols = slice(half * (H // 2), (half + 1) * (H // 2))

@@ -37,7 +37,7 @@ RESET_SUMMED = STREAM.index((RESET, GATE_PASSES - 1)) // ROUND_PASSES + 1
 SMALL_LOADED = 6
 SMALL_LAID_OUT = (10, 12, 14)
 LEAD_IN = 4
-VECTOR_COLS = 352
+LAST_VECTOR_COLS = (256, 352)
 RUN = 4
 
 SLOT_JOINT_H = X_PASSES
@@ -81,7 +81,7 @@ def tile_joint_gru_pa_k_kernel(tc, joint_h, mgn_h, W_r, W_h, U_r, U_h, b_r, b_h,
 
         warm = keep.tile([P, 1], F32)
         nc.vector.memset(warm[:], 0.0)
-        nc.scalar.activation(out=warm[:], in_=warm[:], func=ACT.Tanh)
+        nc.scalar.activation(out=warm[:], in_=warm[:], func=ACT.Sigmoid)
 
         rT = [sums.tile([P, B], F32, name="rT%d" % m) for m in range(H_TILES)]
         cand = sums.tile([B, H], F32)
@@ -96,8 +96,7 @@ def tile_joint_gru_pa_k_kernel(tc, joint_h, mgn_h, W_r, W_h, U_r, U_h, b_r, b_h,
             )
 
         h_grouped = keep.tile([P, B, PACK], BF16, align_bytes=64)
-        half_hT = keep.tile([P, H_TILES, B], F32)
-        half_br = keep.tile([P, H_TILES], F32)
+        br_col = keep.tile([P, H_TILES], F32)
         bh_all = keep.tile([P, H], F32)
 
         def load_small_operands():
@@ -110,12 +109,11 @@ def tile_joint_gru_pa_k_kernel(tc, joint_h, mgn_h, W_r, W_h, U_r, U_h, b_r, b_h,
             for t in range(H_TILES):
                 nc.tensor.transpose(hT_ps[:, t, :], h_sb[:, t * P : (t + 1) * P], ident_bf16[:])
             nc.scalar.copy(out=h_grouped[:], in_=hT_ps[:].rearrange("p t b -> p b t"))
-            nc.scalar.mul(half_hT[:], hT_ps[:], 0.5)
 
         def lay_out_b_r():
             brT_ps = work.tile([P, P], BF16, tag="work")
             nc.tensor.transpose(brT_ps[:], br_rows[:], ident_bf16[:])
-            nc.scalar.mul(half_br[:], brT_ps[:, 0:H_TILES], 0.5)
+            nc.scalar.copy(out=br_col[:], in_=brT_ps[:, 0:H_TILES])
 
         def lay_out_b_h():
             bh_ps = work.tile([P, H], F32, tag="work")
@@ -127,25 +125,25 @@ def tile_joint_gru_pa_k_kernel(tc, joint_h, mgn_h, W_r, W_h, U_r, U_h, b_r, b_h,
                 return (W_r, W_h)[gate][s * K_PASS : (s + 1) * K_PASS, :].rearrange("(p t) n -> p t n", p=P)
             return (U_r, U_h)[gate].rearrange("(t p) n -> p t n", p=P)
 
-        def load_x(m):
+        def load_x(m, pairs):
             x_raw = x_raw_pool.tile([B, X_LOAD_PAIRS * X_PAIR * K_PASS], BF16)
+            width = pairs * X_PAIR * K_PASS
             first_k = m * X_PAIR * K_PASS
-            nc.sync.dma_start(out=x_raw[:], in_=mgn_h[:, first_k : first_k + x_raw.shape[1]])
-            return x_raw
+            nc.sync.dma_start(out=x_raw[:, 0:width], in_=mgn_h[:, first_k : first_k + width])
+            return x_raw, m
 
-        def load_weights(i):
-            w_raw = []
-            for c in range(ROUND_PASSES):
-                gate, s = STREAM[i * ROUND_PASSES + c]
-                w_raw.append(w_raw_pool.tile([P, PACK, H], BF16, name="w_raw%d" % c))
-                nc.sync.dma_start(out=w_raw[c][:], in_=weight_block(gate, s))
+        def load_weights(i, c):
+            gate, s = STREAM[i * ROUND_PASSES + c]
+            w_raw = w_raw_pool.tile([P, PACK, H], BF16, name="w_raw%d" % c)
+            nc.sync.dma_start(out=w_raw[:], in_=weight_block(gate, s))
             return w_raw
 
-        def transpose_x(m, x_raw):
+        def transpose_x(m, loaded):
+            x_raw, first_pair = loaded
             words = x_raw[:].bitcast(F32)
             xT_ps = work.tile([P, X_PAIR, 2, B], F32, tag="work")
             for c in range(X_PAIR):
-                first_word = ((m % X_LOAD_PAIRS) * X_PAIR + c) * (K_PASS // 2)
+                first_word = ((m - first_pair) * X_PAIR + c) * (K_PASS // 2)
                 for u in range(2):
                     nc.tensor.transpose(
                         xT_ps[:, c, u, :],
@@ -214,60 +212,63 @@ def tile_joint_gru_pa_k_kernel(tc, joint_h, mgn_h, W_r, W_h, U_r, U_h, b_r, b_h,
                         stop=(s == GATE_PASSES - 1),
                     )
 
-        def last_round(w_raw):
-            i = ROUNDS - 1
-            w_grouped = w_grouped_pool.tile([P, ROUND_PASSES, H, PACK], BF16, align_bytes=64)
+        def lay_out_last_round(w_raw, w_grouped, c):
+            cols = LAST_VECTOR_COLS[c]
+            regroup(nc.scalar.copy, w_grouped[:, c, cols:, :], w_raw[c][:, :, cols:])
+            regroup(nc.vector.tensor_copy, w_grouped[:, c, :cols, :], w_raw[c][:, :, :cols])
+
+        def finish_last_round(w_grouped):
             w_codes = w_mx_pool.tile([P, ROUND_PASSES * H], U32, align_bytes=64)
             w_scales = w_mx_pool.tile([P, ROUND_PASSES * H], U8, align_bytes=64)
             for c in range(ROUND_PASSES):
-                regroup(nc.scalar.copy, w_grouped[:, c, VECTOR_COLS:, :], w_raw[c][:, :, VECTOR_COLS:])
-                for cols in (slice(0, H // 2), slice(H // 2, VECTOR_COLS)):
-                    regroup(nc.vector.tensor_copy, w_grouped[:, c, cols, :], w_raw[c][:, :, cols])
-                for half in range(2):
-                    first = c * H + half * (H // 2)
-                    quantise_weights(w_codes, w_scales, w_grouped, slice(first, first + H // 2))
-                multiply(i, [c], w_codes, w_scales)
+                quantise_weights(w_codes, w_scales, w_grouped, slice(c * H, (c + 1) * H))
+                multiply(ROUNDS - 1, [c], w_codes, w_scales)
 
-        tanh_rT = keep.tile([P, H_TILES, B], F32)
+        r_T = keep.tile([P, H_TILES, B], F32)
         g_grouped = keep.tile([P, B, PACK], BF16, align_bytes=64)
 
         small_steps = dict(zip(SMALL_LAID_OUT, (lay_out_joint_h, lay_out_b_r, lay_out_b_h)))
         laid_out = None
-        x_raw = None
         xT_next = None
         for i in range(ROUNDS):
             previous = laid_out
-            w_raw = load_weights(i)
+            w_raw = [load_weights(i, 0)]
             if i == 0:
-                x_raw = load_x(0)
-                xT_next = transpose_x(0, x_raw)
+                x_loaded = load_x(0, 1)
+                xT_next = transpose_x(0, x_loaded)
+            w_raw.append(load_weights(i, 1))
             next_pair = X_PAIR_OF_ROUND.get(i + 1)
+            if i == 1:
+                second_pair = load_x(1, 1)
             if next_pair is not None and next_pair % X_LOAD_PAIRS == 0:
-                x_raw = load_x(next_pair)
+                x_loaded = load_x(next_pair, X_LOAD_PAIRS)
             if i == SMALL_LOADED:
                 load_small_operands()
+            if i == 1:
+                xT_next = transpose_x(1, second_pair)
+            xT_ps = xT_next
             if 1 <= i <= LEAD_IN:
                 quantise_and_multiply(i - 1, previous[0], previous[1])
-            xT_ps = xT_next
-            xT_next = None if next_pair is None else transpose_x(next_pair, x_raw)
+            xT_next = None if next_pair is None or i == 0 else transpose_x(next_pair, x_loaded)
             if i < ROUNDS - 1:
                 laid_out = regroup_round(w_raw, xT_ps)
+            else:
+                last_grouped = w_grouped_pool.tile([P, ROUND_PASSES, H, PACK], BF16, align_bytes=64, name="w_grouped")
+                lay_out_last_round(w_raw, last_grouped, 0)
             if i in small_steps:
                 small_steps[i]()
 
             if i == RESET_SUMMED + 1:
                 for m in range(H_TILES):
                     nc.scalar.activation(
-                        out=tanh_rT[:, m, :], in_=rT[m][:], func=ACT.Tanh, bias=half_br[:, m : m + 1], scale=0.5
+                        out=r_T[:, m, :], in_=rT[m][:], func=ACT.Sigmoid, bias=br_col[:, m : m + 1], scale=1.0
                     )
             if i == RESET_SUMMED + 2:
-                nc.vector.scalar_tensor_tensor(
+                nc.vector.tensor_tensor(
                     out=g_grouped[:],
-                    in0=tanh_rT[:].rearrange("p t b -> p b t"),
-                    scalar=1.0,
-                    in1=half_hT[:].rearrange("p t b -> p b t"),
-                    op0=ALU.add,
-                    op1=ALU.mult,
+                    in0=r_T[:].rearrange("p t b -> p b t"),
+                    in1=h_grouped[:],
+                    op=ALU.mult,
                 )
 
             if i > LEAD_IN:
@@ -279,7 +280,8 @@ def tile_joint_gru_pa_k_kernel(tc, joint_h, mgn_h, W_r, W_h, U_r, U_h, b_r, b_h,
             if i == RESET_SUMMED + 2:
                 quantise_activations(SLOT_G, g_grouped[:].rearrange("p b t -> p (b t)"))
 
-        last_round(w_raw)
+        lay_out_last_round(w_raw, last_grouped, 1)
+        finish_last_round(last_grouped)
 
         for half in range(2):
             cols = slice(half * (H // 2), (half + 1) * (H // 2))
@@ -287,4 +289,4 @@ def tile_joint_gru_pa_k_kernel(tc, joint_h, mgn_h, W_r, W_h, U_r, U_h, b_r, b_h,
             nc.vector.tensor_tensor(out=biased[:], in0=cand[:, cols], in1=bh_all[:, cols], op=ALU.add)
             result = keep.tile([B, H // 2], F32, name="result%d" % half)
             nc.scalar.activation(out=result[:], in_=biased[:], func=ACT.Tanh)
-            nc.sync.dma_start(out=out[:, cols], in_=result[:])
+            (nc.sync, nc.scalar)[half].dma_start(out=out[:, cols], in_=result[:])

from contextlib import ExitStack

import concourse.mybir as mybir
from concourse.masks import make_identity

BF16 = mybir.dt.bfloat16
F32 = mybir.dt.float32
U32 = mybir.dt.uint32
U8 = mybir.dt.uint8
FP8X4 = mybir.dt.float8_e4m3fn_x4
ACT = mybir.ActivationFunctionType
ALU = mybir.AluOpType

P = 128
PACK = 4
K_PASS = P * PACK

B, IN, H = 128, 16384, 512
H_TILES = H // P
X_PASSES = IN // K_PASS
GATE_PASSES = X_PASSES + H // K_PASS
RESET, CANDIDATE = 0, 1

RESET_LEAD = 8
STREAM = (
    [(RESET, s) for s in range(RESET_LEAD)]
    + [(gate, s - gate * RESET_LEAD) for s in range(RESET_LEAD, GATE_PASSES) for gate in (RESET, CANDIDATE)]
    + [(CANDIDATE, s) for s in range(GATE_PASSES - RESET_LEAD, GATE_PASSES)]
)

ROUND_PASSES = 2
ROUNDS = 2 * GATE_PASSES // ROUND_PASSES
X_PAIR = 2
X_LOAD_PAIRS = 2
X_PAIR_OF_ROUND = {STREAM.index((RESET, m * X_PAIR)) // ROUND_PASSES: m for m in range(X_PASSES // X_PAIR)}
RESET_SUMMED = STREAM.index((RESET, GATE_PASSES - 1)) // ROUND_PASSES + 1
SMALL_LOADED = 6
SMALL_LAID_OUT = (10, 12, 14)
LEAD_IN = 4
LAST_VECTOR_COLS = (256, 352)
RUN = 4

SLOT_JOINT_H = X_PASSES
SLOT_G = X_PASSES + 1

FLOPS = 2 * B * H * (2 * IN + 2 * H)


def regroup(copy, grouped, rows):
    copy(
        out=grouped.rearrange("p (c i) t -> p c t i", i=RUN),
        in_=rows.rearrange("p t (c i) -> p c t i", i=RUN),
    )


def tile_joint_gru_pa_k_kernel(tc, joint_h, mgn_h, W_r, W_h, U_r, U_h, b_r, b_h, out):
    nc = tc.nc
    with ExitStack() as stack:
        keep = stack.enter_context(tc.tile_pool(name="keep", bufs=1))
        x_raw_pool = stack.enter_context(tc.tile_pool(name="x_raw", bufs=4))
        x_grouped_pool = stack.enter_context(tc.tile_pool(name="x_grouped", bufs=3))
        w_raw_pool = stack.enter_context(tc.tile_pool(name="w_raw", bufs=8))
        w_grouped_pool = stack.enter_context(tc.tile_pool(name="w_grouped", bufs=3))
        w_mx_pool = stack.enter_context(tc.tile_pool(name="w_mx", bufs=3))
        sums = stack.enter_context(tc.psum_pool(name="sums", bufs=1))
        work = stack.enter_context(tc.psum_pool(name="work", bufs=3))
        stack.enter_context(tc.manual_schedule())

        ident_f32 = keep.tile([P, P], F32)
        make_identity(nc, ident_f32[:])
        ident_bf16 = keep.tile([P, P], BF16)
        make_identity(nc, ident_bf16[:])
        ones = keep.tile([P, P], BF16)
        nc.vector.memset(ones[:], 1.0)

        h_sb = keep.tile([B, H], BF16)
        br_rows = keep.tile([P, P], BF16)
        nc.vector.memset(br_rows[:], 0.0)
        bh_rows = keep.tile([P, H], BF16)
        nc.vector.memset(bh_rows[:], 0.0)

        warm = keep.tile([P, 1], F32)
        nc.vector.memset(warm[:], 0.0)
        nc.scalar.activation(out=warm[:], in_=warm[:], func=ACT.Sigmoid)

        rT = [sums.tile([P, B], F32, name="rT%d" % m) for m in range(H_TILES)]
        cand = sums.tile([B, H], F32)

        act_codes = keep.tile([P, (X_PASSES + 2) * B], U32, align_bytes=64)
        act_scales = keep.tile([P, (X_PASSES + 2) * B], U8, align_bytes=64)

        def quantise_activations(first_slot, grouped):
            cols = slice(first_slot * B, first_slot * B + grouped.shape[1] // PACK)
            nc.vector.quantize_mx(
                out=act_codes[:, cols].bitcast(FP8X4), scales=act_scales[:, cols], in_=grouped
            )

        h_grouped = keep.tile([P, B, PACK], BF16, align_bytes=64)
        br_col = keep.tile([P, H_TILES], F32)
        bh_all = keep.tile([P, H], F32)

        def load_small_operands():
            nc.sync.dma_start(out=h_sb[:], in_=joint_h)
            nc.sync.dma_start(out=br_rows[0:H_TILES, :], in_=b_r.rearrange("(t p) -> t p", p=P))
            nc.sync.dma_start(out=bh_rows[0:1, :], in_=b_h.unsqueeze(0))

        def lay_out_joint_h():
            hT_ps = work.tile([P, H_TILES, B], BF16, tag="work")
            for t in range(H_TILES):
                nc.tensor.transpose(hT_ps[:, t, :], h_sb[:, t * P : (t + 1) * P], ident_bf16[:])
            nc.scalar.copy(out=h_grouped[:], in_=hT_ps[:].rearrange("p t b -> p b t"))

        def lay_out_b_r():
            brT_ps = work.tile([P, P], BF16, tag="work")
            nc.tensor.transpose(brT_ps[:], br_rows[:], ident_bf16[:])
            nc.scalar.copy(out=br_col[:], in_=brT_ps[:, 0:H_TILES])

        def lay_out_b_h():
            bh_ps = work.tile([P, H], F32, tag="work")
            nc.tensor.matmul(bh_ps[:], lhsT=ones[:], rhs=bh_rows[:], start=True, stop=True)
            nc.scalar.copy(out=bh_all[:], in_=bh_ps[:])

        def weight_block(gate, s):
            if s < X_PASSES:
                return (W_r, W_h)[gate][s * K_PASS : (s + 1) * K_PASS, :].rearrange("(p t) n -> p t n", p=P)
            return (U_r, U_h)[gate].rearrange("(t p) n -> p t n", p=P)

        def load_x(m, pairs):
            x_raw = x_raw_pool.tile([B, X_LOAD_PAIRS * X_PAIR * K_PASS], BF16)
            width = pairs * X_PAIR * K_PASS
            first_k = m * X_PAIR * K_PASS
            nc.sync.dma_start(out=x_raw[:, 0:width], in_=mgn_h[:, first_k : first_k + width])
            return x_raw, m

        def load_weights(i, c):
            gate, s = STREAM[i * ROUND_PASSES + c]
            w_raw = w_raw_pool.tile([P, PACK, H], BF16, name="w_raw%d" % c)
            nc.sync.dma_start(out=w_raw[:], in_=weight_block(gate, s))
            return w_raw

        def transpose_x(m, loaded):
            x_raw, first_pair = loaded
            words = x_raw[:].bitcast(F32)
            xT_ps = work.tile([P, X_PAIR, 2, B], F32, tag="work")
            for c in range(X_PAIR):
                first_word = ((m - first_pair) * X_PAIR + c) * (K_PASS // 2)
                for u in range(2):
                    nc.tensor.transpose(
                        xT_ps[:, c, u, :],
                        words[:, first_word + u : first_word + K_PASS // 2 : 2],
                        ident_f32[:],
                    )
            return xT_ps

        def regroup_round(w_raw, xT_ps):
            w_grouped = w_grouped_pool.tile([P, ROUND_PASSES, H, PACK], BF16, align_bytes=64)
            regroup(nc.scalar.copy, w_grouped[:, 0, :, :], w_raw[0][:])
            regroup(nc.vector.tensor_copy, w_grouped[:, 1, :, :], w_raw[1][:])

            x_grouped = None
            if xT_ps is not None:
                x_grouped = x_grouped_pool.tile([P, X_PAIR * B * PACK], BF16, align_bytes=64)
                nc.scalar.copy(
                    out=x_grouped[:].bitcast(F32).rearrange("p (c b u) -> p c b u", c=X_PAIR, u=2),
                    in_=xT_ps[:].rearrange("p c u b -> p c b u"),
                )
            return w_grouped, x_grouped

        def quantise_weights(w_codes, w_scales, w_grouped, cols):
            nc.vector.quantize_mx(
                out=w_codes[:, cols].bitcast(FP8X4),
                scales=w_scales[:, cols],
                in_=w_grouped[:].rearrange("p c n t -> p (c n t)")[:, cols.start * PACK : cols.stop * PACK],
            )

        def quantise_and_multiply(i, w_grouped, x_grouped):
            w_codes = w_mx_pool.tile([P, ROUND_PASSES * H], U32, align_bytes=64)
            w_scales = w_mx_pool.tile([P, ROUND_PASSES * H], U8, align_bytes=64)
            width = H if i < LEAD_IN else ROUND_PASSES * H
            for first in range(0, ROUND_PASSES * H, width):
                quantise_weights(w_codes, w_scales, w_grouped, slice(first, first + width))
            if x_grouped is not None:
                quantise_activations(X_PAIR_OF_ROUND[i] * X_PAIR, x_grouped[:])
            multiply(i, range(ROUND_PASSES), w_codes, w_scales)

        def multiply(i, passes, w_codes, w_scales):
            for c in passes:
                gate, s = STREAM[i * ROUND_PASSES + c]
                slot = s if s < X_PASSES else (SLOT_JOINT_H, SLOT_G)[gate]
                a_cols = slice(slot * B, (slot + 1) * B)
                if gate == RESET:
                    for m in range(H_TILES):
                        w_cols = slice(c * H + m * P, c * H + (m + 1) * P)
                        nc.tensor.matmul_mx(
                            out=rT[m][:],
                            lhsT=w_codes[:, w_cols].bitcast(FP8X4),
                            lhsT_scale=w_scales[:, w_cols],
                            rhs=act_codes[:, a_cols].bitcast(FP8X4),
                            rhs_scale=act_scales[:, a_cols],
                            start=(s == 0),
                            stop=(s == GATE_PASSES - 1),
                        )
                else:
                    w_cols = slice(c * H, (c + 1) * H)
                    nc.tensor.matmul_mx(
                        out=cand[:],
                        lhsT=act_codes[:, a_cols].bitcast(FP8X4),
                        lhsT_scale=act_scales[:, a_cols],
                        rhs=w_codes[:, w_cols].bitcast(FP8X4),
                        rhs_scale=w_scales[:, w_cols],
                        start=(s == 0),
                        stop=(s == GATE_PASSES - 1),
                    )

        def lay_out_last_round(w_raw, w_grouped, c):
            cols = LAST_VECTOR_COLS[c]
            regroup(nc.scalar.copy, w_grouped[:, c, cols:, :], w_raw[c][:, :, cols:])
            regroup(nc.vector.tensor_copy, w_grouped[:, c, :cols, :], w_raw[c][:, :, :cols])

        def finish_last_round(w_grouped):
            w_codes = w_mx_pool.tile([P, ROUND_PASSES * H], U32, align_bytes=64)
            w_scales = w_mx_pool.tile([P, ROUND_PASSES * H], U8, align_bytes=64)
            for c in range(ROUND_PASSES):
                quantise_weights(w_codes, w_scales, w_grouped, slice(c * H, (c + 1) * H))
                multiply(ROUNDS - 1, [c], w_codes, w_scales)

        r_T = keep.tile([P, H_TILES, B], F32)
        g_grouped = keep.tile([P, B, PACK], BF16, align_bytes=64)

        small_steps = dict(zip(SMALL_LAID_OUT, (lay_out_joint_h, lay_out_b_r, lay_out_b_h)))
        laid_out = None
        xT_next = None
        for i in range(ROUNDS):
            previous = laid_out
            w_raw = [load_weights(i, 0)]
            if i == 0:
                x_loaded = load_x(0, 1)
                xT_next = transpose_x(0, x_loaded)
            w_raw.append(load_weights(i, 1))
            next_pair = X_PAIR_OF_ROUND.get(i + 1)
            if i == 1:
                second_pair = load_x(1, 1)
            if next_pair is not None and next_pair % X_LOAD_PAIRS == 0:
                x_loaded = load_x(next_pair, X_LOAD_PAIRS)
            if i == SMALL_LOADED:
                load_small_operands()
            if i == 1:
                xT_next = transpose_x(1, second_pair)
            xT_ps = xT_next
            if 1 <= i <= LEAD_IN:
                quantise_and_multiply(i - 1, previous[0], previous[1])
            xT_next = None if next_pair is None or i == 0 else transpose_x(next_pair, x_loaded)
            if i < ROUNDS - 1:
                laid_out = regroup_round(w_raw, xT_ps)
            else:
                last_grouped = w_grouped_pool.tile([P, ROUND_PASSES, H, PACK], BF16, align_bytes=64, name="w_grouped")
                lay_out_last_round(w_raw, last_grouped, 0)
            if i in small_steps:
                small_steps[i]()

            if i == RESET_SUMMED + 1:
                for m in range(H_TILES):
                    nc.scalar.activation(
                        out=r_T[:, m, :], in_=rT[m][:], func=ACT.Sigmoid, bias=br_col[:, m : m + 1], scale=1.0
                    )
            if i == RESET_SUMMED + 2:
                nc.vector.tensor_tensor(
                    out=g_grouped[:],
                    in0=r_T[:].rearrange("p t b -> p b t"),
                    in1=h_grouped[:],
                    op=ALU.mult,
                )

            if i > LEAD_IN:
                quantise_and_multiply(i - 1, previous[0], previous[1])

            if i == SMALL_LAID_OUT[0] + 1:
                quantise_activations(SLOT_JOINT_H, h_grouped[:].rearrange("p b t -> p (b t)"))

            if i == RESET_SUMMED + 2:
                quantise_activations(SLOT_G, g_grouped[:].rearrange("p b t -> p (b t)"))

        lay_out_last_round(w_raw, last_grouped, 1)
        finish_last_round(last_grouped)

        for half in range(2):
            cols = slice(half * (H // 2), (half + 1) * (H // 2))
            biased = keep.tile([B, H // 2], F32, name="biased%d" % half)
            nc.vector.tensor_tensor(out=biased[:], in0=cand[:, cols], in1=bh_all[:, cols], op=ALU.add)
            result = keep.tile([B, H // 2], F32, name="result%d" % half)
            nc.scalar.activation(out=result[:], in_=biased[:], func=ACT.Tanh)
            (nc.sync, nc.scalar)[half].dma_start(out=out[:, cols], in_=result[:])
